import numpy as np
import ml_dtypes


def mxq(x, axis, fmt="e4m3"):
    dtype, down = {"e4m3": (ml_dtypes.float8_e4m3fn, 7), "e5m2": (ml_dtypes.float8_e5m2, 14)}[fmt]
    v = np.moveaxis(np.asarray(x, np.float32).astype(ml_dtypes.bfloat16).astype(np.float64), axis, -1)
    blocks = v.reshape(v.shape[:-1] + (-1, 32))
    amax = np.abs(blocks).max(-1, keepdims=True)
    byte = np.maximum(np.where(amax > 0, np.frexp(amax)[1] - 1 + 127, 0) - down, 1)
    scale = np.exp2(byte - 127.0)
    codes = (blocks / scale).astype(np.float32).astype(dtype).astype(np.float64)
    return np.moveaxis((codes * scale).reshape(v.shape), -1, axis)


WIDE = False


def mx_kscale(k):
    if not WIDE:
        return np.ones(k)
    levels = np.array([10, -10, 5, -5, 0])
    a = np.random.permutation(np.resize(levels, k // 512 * 4)).reshape(k // 512, 4)
    idx = np.arange(k)
    return np.exp2(a[idx // 512, idx % 128 // 32])


BF16 = ml_dtypes.bfloat16


def bf(x):
    return np.asarray(x, np.float32).astype(BF16)


def f64(x):
    return np.asarray(x).astype(np.float64)


T, D, H, C = 8192, 512, 4, 32
E = H * C
EPS = 1e-6
BASE = 10000.0


def rope_tables():
    inv_freq = 1.0 / BASE ** (np.arange(0, C, 2) / C)
    freqs = np.arange(T)[:, None] * inv_freq[None, :]
    return np.sin(freqs), np.cos(freqs)


def rotate_every_two(v):
    return np.stack((-v[..., 1::2], v[..., ::2]), axis=-1).reshape(v.shape)


def apply_rope(v, sin, cos):
    sin = np.repeat(sin, 2, axis=-1)[None]
    cos = np.repeat(cos, 2, axis=-1)[None]
    return v * cos + rotate_every_two(v) * sin


def layernorm(v, w):
    mu = v.mean(-1, keepdims=True)
    var = v.var(-1, keepdims=True)
    return (v - mu) / np.sqrt(var + EPS) * w


def heads(v):
    return v.reshape(T, H, C).transpose(1, 0, 2)


def setup_inputs():
    s = mx_kscale(D)
    return {"x": bf(np.random.standard_normal((T, D)) * s),
            "W_attn": bf(np.random.standard_normal((3 * E, D)) / np.sqrt(D) / s[None, :]),
            "b_attn": bf(np.random.standard_normal(3 * E) * 0.3),
            "q_ln_w": bf(1.0 + 0.2 * np.random.standard_normal(C)),
            "k_ln_w": bf(1.0 + 0.2 * np.random.standard_normal(C))}


def reference(x, W_attn, b_attn, q_ln_w, k_ln_w):
    xq = mxq(f64(x), 1, "e4m3")
    wq, wk, wv = np.split(f64(W_attn), 3, axis=0)
    bq, bk, bv = np.split(f64(b_attn), 3)
    q = heads((xq @ mxq(wq, 1, "e4m3").T) + bq)
    k = heads((xq @ mxq(wk, 1, "e4m3").T) + bk)
    v = heads((xq @ mxq(wv, 1, "e4m3").T) + bv)
    q = layernorm(q, f64(q_ln_w))
    k = layernorm(k, f64(k_ln_w))
    sin, cos = rope_tables()
    return apply_rope(q, sin, cos), apply_rope(k, sin, cos), v

@@ -1,0 +1,367 @@
+from contextlib import ExitStack
+
+import concourse.mybir as mybir
+from concourse.masks import make_identity
+
+F32 = mybir.dt.float32
+BF16 = mybir.dt.bfloat16
+I32 = mybir.dt.int32
+U32 = mybir.dt.uint32
+U8 = mybir.dt.uint8
+FP8X4 = mybir.dt.float8_e4m3fn_x4
+ALU = mybir.AluOpType
+ACT = mybir.ActivationFunctionType
+
+T, D, H, C = 8192, 512, 4, 32
+E = H * C
+EPS = 1e-6
+BASE = 10000.0
+PI = 3.141592653589793
+
+P = 128
+SUB = 8
+CHUNK = P * SUB
+CHUNKS = T // CHUNK
+POS = CHUNKS * SUB
+PAIRS = C // 2
+GROUPS = 2 * H * SUB
+X_BUFS = 6
+ROUND = 12582912.0
+
+FLOPS = 2 * T * D * 3 * E
+
+
+def split_frequency(pair):
+    turns = BASE ** (-pair / PAIRS) / (2.0 * PI)
+    scale = 1.0
+    while turns * scale < 1024.0:
+        scale = scale * 2.0
+    high = round(turns * scale) / scale
+    return high, turns - high
+
+
+def tile_causalselfattention_pa_t_kernel(
+    tc, x, W_attn, b_attn, q_ln_w, k_ln_w, out_0, out_1, out_2
+):
+    nc = tc.nc
+    with ExitStack() as ctx:
+        const = ctx.enter_context(tc.tile_pool(name="const", bufs=1))
+        setup = ctx.enter_context(tc.tile_pool(name="setup", bufs=1))
+        xpool = ctx.enter_context(tc.tile_pool(name="xpool", bufs=X_BUFS))
+        quant = ctx.enter_context(tc.tile_pool(name="quant", bufs=2))
+        work = ctx.enter_context(tc.tile_pool(name="work", bufs=2))
+        small = ctx.enter_context(tc.tile_pool(name="small", bufs=2))
+        ps_t = ctx.enter_context(tc.psum_pool(name="ps_t", bufs=2))
+        ps_qk = ctx.enter_context(tc.psum_pool(name="ps_qk", bufs=4))
+        ps_v = ctx.enter_context(tc.psum_pool(name="ps_v", bufs=2))
+        ctx.enter_context(tc.manual_schedule())
+
+        x_rows = {}
+        grouped = {}
+        codes = {}
+        scales = {}
+        acc_qk = {}
+        acc_v = {}
+        u_qk = {}
+        stats = {}
+        std = {}
+        rstd = {}
+        shift = {}
+        straight = {}
+        crossed = {}
+
+        def load(g):
+            x_rows[g] = xpool.tile([P, SUB, D], BF16, name="x_rows")
+            nc.sync.dma_start(
+                out=x_rows[g][:],
+                in_=x[g * CHUNK : (g + 1) * CHUNK, :].rearrange("(p s) k -> p s k", s=SUB),
+            )
+
+        def turn(g):
+            grouped[g] = quant.tile([P, CHUNK * 4], BF16, align_bytes=64, name="grouped")
+            words = grouped[g][:].bitcast(F32).rearrange("p (s m u) -> p s m u", s=SUB, u=2)
+            for b in range(SUB // 2):
+                xt = ps_t.tile([P, 2, 2, P], F32, tag="xt")
+                for s in range(2):
+                    for u in range(2):
+                        nc.tensor.transpose(
+                            xt[:, s, u, :],
+                            x_rows[g][:, 2 * b + s, :].bitcast(F32)[:, u * P : (u + 1) * P],
+                            ident[:],
+                        )
+                nc.scalar.copy(
+                    out=words[:, 2 * b : 2 * b + 2, :, :],
+                    in_=xt[:].rearrange("p s u m -> p s m u"),
+                )
+            if g + X_BUFS < CHUNKS:
+                load(g + X_BUFS)
+
+        load(0)
+        w_rows = setup.tile([P, 3, D], BF16)
+        nc.sync.dma_start(out=w_rows[:], in_=W_attn.rearrange("(a p) k -> p a k", p=P))
+        for g in range(1, X_BUFS):
+            load(g)
+        vectors = setup.tile([P, 4 * E], BF16)
+        nc.vector.memset(vectors[:], 0.0)
+        nc.scalar.dma_start(out=vectors[0:1, 0 : 3 * E], in_=b_attn.rearrange("(o n) -> o n", o=1))
+        nc.scalar.dma_start(
+            out=vectors[0:1, 3 * E : 3 * E + C], in_=q_ln_w.rearrange("(o n) -> o n", o=1)
+        )
+        nc.scalar.dma_start(
+            out=vectors[0:1, 3 * E + C : 3 * E + 2 * C], in_=k_ln_w.rearrange("(o n) -> o n", o=1)
+        )
+        ones = setup.tile([P, P], BF16)
+        nc.vector.memset(ones[:], 1.0)
+        eps = const.tile([P, 1], F32)
+        nc.vector.memset(eps[:], EPS)
+        ident = const.tile([P, P], F32)
+        make_identity(nc, ident[:])
+        pos_i = setup.tile([P, POS], I32)
+        nc.gpsimd.iota(pos_i[:], pattern=[[CHUNK, CHUNKS], [1, SUB]], base=0, channel_multiplier=SUB)
+
+        pos = setup.tile([P, POS], F32)
+        nc.vector.tensor_copy(out=pos[:], in_=pos_i[:])
+        whole = setup.tile([P, PAIRS, POS], F32)
+        for j in range(PAIRS):
+            high, low = split_frequency(j)
+            nc.vector.tensor_scalar(
+                out=whole[:, j, :], in0=pos[:], scalar1=high, scalar2=ROUND,
+                op0=ALU.mult, op1=ALU.add,
+            )
+        nc.vector.tensor_scalar_sub(out=whole[:], in0=whole[:], scalar1=ROUND)
+        turns = setup.tile([P, 2, PAIRS, POS], F32)
+        for j in range(PAIRS):
+            high, low = split_frequency(j)
+            nc.vector.scalar_tensor_tensor(
+                out=whole[:, j, :], in0=pos[:], scalar=high, in1=whole[:, j, :],
+                op0=ALU.mult, op1=ALU.subtract,
+            )
+            nc.vector.scalar_tensor_tensor(
+                out=turns[:, 0, j, :], in0=pos[:], scalar=low, in1=whole[:, j, :],
+                op0=ALU.mult, op1=ALU.add,
+            )
+        nc.vector.tensor_scalar_add(out=turns[:, 1, :, :], in0=turns[:, 0, :, :], scalar1=0.25)
+        nearest = setup.tile([P, 2, PAIRS, POS], F32)
+        nc.vector.tensor_scalar(
+            out=nearest[:], in0=turns[:], scalar1=ROUND, scalar2=ROUND,
+            op0=ALU.add, op1=ALU.subtract,
+        )
+        nc.vector.tensor_sub(out=turns[:], in0=turns[:], in1=nearest[:])
+        turn(0)
+        trig = setup.tile([P, 2, POS, PAIRS], F32)
+        for s in range(2):
+            nc.scalar.activation(
+                out=trig[:, s, :, :], in_=turns[:, s, :, :].rearrange("p j i -> p i j"),
+                func=ACT.Sin, scale=2.0 * PI,
+            )
+
+        w_grouped = setup.tile([P, 3 * E * 4], BF16, align_bytes=64)
+        w_words = w_grouped[:].bitcast(F32).rearrange("p (a r u) -> p a r u", a=3, u=2)
+        w_codes = const.tile([P, 3 * E], U32, align_bytes=64)
+        w_scales = const.tile([P, 3 * E], U8, align_bytes=64)
+        for a in range(3):
+            wt = ps_t.tile([P, 2, 2, P], F32, tag="xt")
+            for u in range(2):
+                nc.tensor.transpose(
+                    wt[:, 0, u, :], w_rows[:, a, :].bitcast(F32)[:, u * P : (u + 1) * P], ident[:]
+                )
+            if a < 2:
+                for e in range(2):
+                    nc.vector.tensor_copy(
+                        out=w_words[:, a, :, :].rearrange("p (h e j) u -> p h e j u", h=H, e=2)[
+                            :, :, e, :, :
+                        ],
+                        in_=wt[:, 0, :, :].rearrange("p u (h j e) -> p h e j u", h=H, e=2)[
+                            :, :, e, :, :
+                        ],
+                    )
+            else:
+                nc.vector.tensor_copy(
+                    out=w_words[:, a, :, :], in_=wt[:, 0, :, :].rearrange("p u r -> p r u")
+                )
+        nc.vector.quantize_mx(
+            out=w_codes[:, 0 : 2 * E].bitcast(FP8X4),
+            scales=w_scales[:, 0 : 2 * E],
+            in_=w_grouped[:, 0 : 2 * E * 4],
+        )
+        nc.vector.quantize_mx(
+            out=w_codes[:, 2 * E : 3 * E].bitcast(FP8X4),
+            scales=w_scales[:, 2 * E : 3 * E],
+            in_=w_grouped[:, 2 * E * 4 : 3 * E * 4],
+        )
+
+        spread = ps_qk.tile([P, 4 * E], F32, tag="acc")
+        nc.tensor.matmul(out=spread[:], lhsT=ones[:], rhs=vectors[:], start=True, stop=True)
+        bias = const.tile([P, 3 * E], F32)
+        nc.vector.tensor_copy(
+            out=bias[:, 0 : 2 * E].rearrange("p (g e j) -> p g e j", e=2, j=PAIRS),
+            in_=spread[:, 0 : 2 * E].rearrange("p (g j e) -> p g e j", e=2, j=PAIRS),
+        )
+        nc.vector.tensor_copy(out=bias[:, 2 * E : 3 * E], in_=spread[:, 2 * E : 3 * E])
+        gain = const.tile([P, 2, 2, PAIRS], F32)
+        nc.vector.tensor_copy(
+            out=gain[:],
+            in_=spread[:, 3 * E : 3 * E + 2 * C].rearrange("p (t j e) -> p t e j", t=2, e=2),
+        )
+        cross = const.tile([P, 2, 2, PAIRS], F32)
+        nc.vector.tensor_scalar_mul(out=cross[:, :, 0, :], in0=gain[:, :, 1, :], scalar1=-1.0)
+        nc.vector.tensor_copy(out=cross[:, :, 1, :], in_=gain[:, :, 0, :])
+
+        own = const.tile([P, 2, POS, 2, PAIRS], F32)
+        other = const.tile([P, 2, 2, POS, PAIRS], F32)
+        for t in range(2):
+            for e in range(2):
+                nc.gpsimd.tensor_mul(
+                    out=other[:, e, t, :, :],
+                    in0=trig[:, 0, :, :],
+                    in1=cross[:, t, e, :].unsqueeze(1).to_broadcast([P, POS, PAIRS]),
+                )
+            nc.gpsimd.tensor_mul(
+                out=own[:, t, :, :, :],
+                in0=trig[:, 1, :, :].unsqueeze(2).to_broadcast([P, POS, 2, PAIRS]),
+                in1=gain[:, t, :, :].unsqueeze(1).to_broadcast([P, POS, 2, PAIRS]),
+            )
+
+        def project(g):
+            codes[g] = quant.tile([P, CHUNK], U32, align_bytes=64, name="codes")
+            scales[g] = quant.tile([P, CHUNK], U8, align_bytes=64, name="scales")
+            nc.vector.quantize_mx(
+                out=codes[g][:].bitcast(FP8X4), scales=scales[g][:], in_=grouped[g][:]
+            )
+            acc_qk[g] = []
+            for b in range(SUB // 2):
+                acc = ps_qk.tile([P, 2, 2 * E], F32, tag="acc")
+                for s in range(2):
+                    cols = slice((2 * b + s) * P, (2 * b + s + 1) * P)
+                    nc.tensor.matmul_mx(
+                        out=acc[:, s, :],
+                        lhsT=codes[g][:, cols].bitcast(FP8X4), lhsT_scale=scales[g][:, cols],
+                        rhs=w_codes[:, 0 : 2 * E].bitcast(FP8X4), rhs_scale=w_scales[:, 0 : 2 * E],
+                        start=True, stop=True,
+                    )
+                acc_qk[g].append(acc)
+            acc_v[g] = []
+            for b in range(SUB // 4):
+                acc = ps_v.tile([P, 4, E], F32, tag="acc_v")
+                for s in range(4):
+                    cols = slice((4 * b + s) * P, (4 * b + s + 1) * P)
+                    nc.tensor.matmul_mx(
+                        out=acc[:, s, :],
+                        lhsT=codes[g][:, cols].bitcast(FP8X4), lhsT_scale=scales[g][:, cols],
+                        rhs=w_codes[:, 2 * E : 3 * E].bitcast(FP8X4),
+                        rhs_scale=w_scales[:, 2 * E : 3 * E],
+                        start=True, stop=True,
+                    )
+                acc_v[g].append(acc)
+
+        def add_bias(g):
+            u_qk[g] = work.tile([P, 2 * H, SUB, C], F32, name="u_qk")
+            for b in range(SUB // 2):
+                nc.vector.tensor_add(
+                    out=u_qk[g][:, :, 2 * b : 2 * b + 2, :],
+                    in0=acc_qk[g][b][:].rearrange("p s (g c) -> p g s c", c=C),
+                    in1=bias[:, 0 : 2 * E].rearrange("p (g c) -> p g c", c=C).unsqueeze(2)
+                    .to_broadcast([P, 2 * H, 2, C]),
+                )
+            v_out = work.tile([P, H, SUB, C], F32)
+            for b in range(SUB // 4):
+                nc.vector.tensor_add(
+                    out=v_out[:, :, 4 * b : 4 * b + 4, :],
+                    in0=acc_v[g][b][:].rearrange("p s (h c) -> p h s c", c=C),
+                    in1=bias[:, 2 * E : 3 * E].rearrange("p (h c) -> p h c", c=C).unsqueeze(2)
+                    .to_broadcast([P, H, 4, C]),
+                )
+            nc.sync.dma_start(
+                out=out_2[:, g * CHUNK : (g + 1) * CHUNK, :].rearrange(
+                    "h (p s) c -> p h (s c)", s=SUB
+                ),
+                in_=v_out[:].rearrange("p h s c -> p h (s c)"),
+            )
+
+        def measure(g):
+            pairs_of_groups = u_qk[g][:].rearrange("p g s c -> p (g s) c").rearrange(
+                "p (n two) c -> p n c two", two=2
+            )
+            stats[g] = small.tile([P, GROUPS, 3], F32, name="stats")
+            for n in range(GROUPS // 2):
+                nc.vector.bn_stats(
+                    out=stats[g][:, 2 * n : 2 * n + 2, :].rearrange("p two k -> p (two k)"),
+                    in_=pairs_of_groups[:, n, :, :],
+                )
+            std[g] = small.tile([P, GROUPS], F32, name="std")
+            nc.scalar.activation(
+                out=std[g][:], in_=stats[g][:, :, 2], func=ACT.Sqrt, scale=1.0 / C, bias=eps[:]
+            )
+
+        def invert(g):
+            rstd[g] = small.tile([P, GROUPS], F32, name="rstd")
+            nc.vector.reciprocal(out=rstd[g][:], in_=std[g][:])
+            shift[g] = small.tile([P, GROUPS], F32, name="shift")
+            nc.vector.scalar_tensor_tensor(
+                out=shift[g][:], in0=stats[g][:, :, 1], scalar=-1.0, in1=rstd[g][:],
+                op0=ALU.mult, op1=ALU.mult,
+            )
+
+        def normalise(g):
+            groups = u_qk[g][:].rearrange("p g s c -> p (g s) c")
+            for i in range(GROUPS):
+                nc.scalar.activation(
+                    out=groups[:, i, :], in_=groups[:, i, :], func=ACT.Identity,
+                    scale=rstd[g][:, i : i + 1], bias=shift[g][:, i : i + 1],
+                )
+
+        def rotate_partner(g):
+            normed = u_qk[g][:].rearrange("p g s (e j) -> p (g s) e j", e=2)
+            crossed[g] = work.tile([P, GROUPS, 2, PAIRS], F32, name="crossed")
+            for e in range(2):
+                nc.gpsimd.tensor_mul(
+                    out=crossed[g][:, :, e, :].rearrange("p (t h s) j -> p t h s j", t=2, h=H),
+                    in0=normed[:, :, 1 - e, :].rearrange("p (t h s) j -> p t h s j", t=2, h=H),
+                    in1=other[:, e, :, g * SUB : (g + 1) * SUB, :].unsqueeze(2)
+                    .to_broadcast([P, 2, H, SUB, PAIRS]),
+                )
+
+        def rotate_own(g):
+            straight[g] = work.tile([P, GROUPS, 2, PAIRS], F32, name="straight")
+            nc.vector.tensor_mul(
+                out=straight[g][:].rearrange("p (t h s) e j -> p t h (s e j)", t=2, h=H),
+                in0=u_qk[g][:].rearrange("p (t h) s c -> p t h (s c)", t=2),
+                in1=own[:, :, g * SUB : (g + 1) * SUB, :, :].rearrange("p t s e j -> p t (s e j)")
+                .unsqueeze(2).to_broadcast([P, 2, H, SUB * C]),
+            )
+
+        def finish(g):
+            qk_out = work.tile([P, GROUPS, PAIRS, 2], F32)
+            nc.vector.tensor_add(
+                out=qk_out[:],
+                in0=straight[g][:].rearrange("p i e j -> p i j e"),
+                in1=crossed[g][:].rearrange("p i e j -> p i j e"),
+            )
+            for t, dest in enumerate((out_0, out_1)):
+                nc.sync.dma_start(
+                    out=dest[:, g * CHUNK : (g + 1) * CHUNK, :].rearrange(
+                        "h (p s) c -> p h (s c)", s=SUB
+                    ),
+                    in_=qk_out[:, t * H * SUB : (t + 1) * H * SUB, :, :].rearrange(
+                        "p (h s) j e -> p h (s j e)", h=H
+                    ),
+                )
+
+        for i in range(-1, CHUNKS + 1):
+            if 0 <= i - 1:
+                normalise(i - 1)
+            if i + 2 < CHUNKS:
+                turn(i + 2)
+            if 0 <= i < CHUNKS:
+                add_bias(i)
+            if i + 1 < CHUNKS:
+                project(i + 1)
+            if 0 <= i < CHUNKS:
+                measure(i)
+            if 0 <= i - 1:
+                rotate_partner(i - 1)
+                rotate_own(i - 1)
+            if 0 <= i < CHUNKS:
+                invert(i)
+            if 0 <= i - 1:
+                finish(i - 1)

@@ -349,19 +349,17 @@ def tile_causalselfattention_pa_t_kernel(
 
         for i in range(-1, CHUNKS + 1):
             if 0 <= i - 1:
-                normalise(i - 1)
+                rotate_partner(i - 1)
             if i + 2 < CHUNKS:
                 turn(i + 2)
             if 0 <= i < CHUNKS:
                 add_bias(i)
+                measure(i)
             if i + 1 < CHUNKS:
                 project(i + 1)
             if 0 <= i < CHUNKS:
-                measure(i)
-            if 0 <= i - 1:
-                rotate_partner(i - 1)
-                rotate_own(i - 1)
-            if 0 <= i < CHUNKS:
                 invert(i)
+                normalise(i)
             if 0 <= i - 1:
+                rotate_own(i - 1)
                 finish(i - 1)

@@ -25,7 +25,7 @@ CHUNKS = T // CHUNK
 POS = CHUNKS * SUB
 PAIRS = C // 2
 GROUPS = 2 * H * SUB
-X_BUFS = 6
+X_BUFS = 5
 ROUND = 12582912.0
 
 FLOPS = 2 * T * D * 3 * E
@@ -52,8 +52,9 @@ def tile_causalselfattention_pa_t_kernel(
         work = ctx.enter_context(tc.tile_pool(name="work", bufs=2))
         small = ctx.enter_context(tc.tile_pool(name="small", bufs=2))
         ps_t = ctx.enter_context(tc.psum_pool(name="ps_t", bufs=2))
-        ps_qk = ctx.enter_context(tc.psum_pool(name="ps_qk", bufs=4))
-        ps_v = ctx.enter_context(tc.psum_pool(name="ps_v", bufs=2))
+        ps_qk = ctx.enter_context(tc.psum_pool(name="ps_qk", bufs=3))
+        ps_vt = ctx.enter_context(tc.psum_pool(name="ps_vt", bufs=2))
+        ps_vb = ctx.enter_context(tc.psum_pool(name="ps_vb", bufs=1))
         ctx.enter_context(tc.manual_schedule())
 
         x_rows = {}
@@ -192,12 +193,18 @@ def tile_causalselfattention_pa_t_kernel(
 
         spread = ps_qk.tile([P, 4 * E], F32, tag="acc")
         nc.tensor.matmul(out=spread[:], lhsT=ones[:], rhs=vectors[:], start=True, stop=True)
-        bias = const.tile([P, 3 * E], F32)
+        bias = const.tile([P, 2 * E], F32)
         nc.vector.tensor_copy(
-            out=bias[:, 0 : 2 * E].rearrange("p (g e j) -> p g e j", e=2, j=PAIRS),
+            out=bias[:].rearrange("p (g e j) -> p g e j", e=2, j=PAIRS),
             in_=spread[:, 0 : 2 * E].rearrange("p (g j e) -> p g e j", e=2, j=PAIRS),
         )
-        nc.vector.tensor_copy(out=bias[:, 2 * E : 3 * E], in_=spread[:, 2 * E : 3 * E])
+        column = ps_vb.tile([P, 4, P], F32, tag="v_back")
+        nc.tensor.matmul(
+            out=column[:, 0, 0:C], lhsT=vectors[:, 2 * E : 3 * E], rhs=ones[:, 0:C],
+            start=True, stop=True,
+        )
+        bias_v = const.tile([P, 1], F32)
+        nc.vector.tensor_copy(out=bias_v[:], in_=column[:, 0, 0:1])
         gain = const.tile([P, 2, 2, PAIRS], F32)
         nc.vector.tensor_copy(
             out=gain[:],
@@ -228,6 +235,18 @@ def tile_causalselfattention_pa_t_kernel(
             nc.vector.quantize_mx(
                 out=codes[g][:].bitcast(FP8X4), scales=scales[g][:], in_=grouped[g][:]
             )
+            acc_v[g] = []
+            for b in range(SUB // 4):
+                acc = ps_vt.tile([P, 4 * P], F32, tag="v_t")
+                cols = slice(4 * b * P, 4 * (b + 1) * P)
+                nc.tensor.matmul_mx(
+                    out=acc[:],
+                    lhsT=w_codes[:, 2 * E : 3 * E].bitcast(FP8X4),
+                    lhsT_scale=w_scales[:, 2 * E : 3 * E],
+                    rhs=codes[g][:, cols].bitcast(FP8X4), rhs_scale=scales[g][:, cols],
+                    start=True, stop=True,
+                )
+                acc_v[g].append(acc)
             acc_qk[g] = []
             for b in range(SUB // 2):
                 acc = ps_qk.tile([P, 2, 2 * E], F32, tag="acc")
@@ -240,19 +259,6 @@ def tile_causalselfattention_pa_t_kernel(
                         start=True, stop=True,
                     )
                 acc_qk[g].append(acc)
-            acc_v[g] = []
-            for b in range(SUB // 4):
-                acc = ps_v.tile([P, 4, E], F32, tag="acc_v")
-                for s in range(4):
-                    cols = slice((4 * b + s) * P, (4 * b + s + 1) * P)
-                    nc.tensor.matmul_mx(
-                        out=acc[:, s, :],
-                        lhsT=codes[g][:, cols].bitcast(FP8X4), lhsT_scale=scales[g][:, cols],
-                        rhs=w_codes[:, 2 * E : 3 * E].bitcast(FP8X4),
-                        rhs_scale=w_scales[:, 2 * E : 3 * E],
-                        start=True, stop=True,
-                    )
-                acc_v[g].append(acc)
 
         def add_bias(g):
             u_qk[g] = work.tile([P, 2 * H, SUB, C], F32, name="u_qk")
@@ -260,16 +266,25 @@ def tile_causalselfattention_pa_t_kernel(
                 nc.vector.tensor_add(
                     out=u_qk[g][:, :, 2 * b : 2 * b + 2, :],
                     in0=acc_qk[g][b][:].rearrange("p s (g c) -> p g s c", c=C),
-                    in1=bias[:, 0 : 2 * E].rearrange("p (g c) -> p g c", c=C).unsqueeze(2)
+                    in1=bias[:].rearrange("p (g c) -> p g c", c=C).unsqueeze(2)
                     .to_broadcast([P, 2 * H, 2, C]),
+                )
+
+        def value(g):
+            v_turned = work.tile([P, SUB, P], F32)
+            for b in range(SUB // 4):
+                nc.scalar.activation(
+                    out=v_turned[:, 4 * b : 4 * b + 4, :].rearrange("p s m -> p (s m)"),
+                    in_=acc_v[g][b][:], func=ACT.Identity, bias=bias_v[:],
                 )
             v_out = work.tile([P, H, SUB, C], F32)
             for b in range(SUB // 4):
-                nc.vector.tensor_add(
+                v_back = ps_vb.tile([P, 4, P], F32, tag="v_back")
+                for s in range(4):
+                    nc.tensor.transpose(v_back[:, s, :], v_turned[:, 4 * b + s, :], ident[:])
+                nc.scalar.copy(
                     out=v_out[:, :, 4 * b : 4 * b + 4, :],
-                    in0=acc_v[g][b][:].rearrange("p s (h c) -> p h s c", c=C),
-                    in1=bias[:, 2 * E : 3 * E].rearrange("p (h c) -> p h c", c=C).unsqueeze(2)
-                    .to_broadcast([P, H, 4, C]),
+                    in_=v_back[:].rearrange("p s (h c) -> p h s c", c=C),
                 )
             nc.sync.dma_start(
                 out=out_2[:, g * CHUNK : (g + 1) * CHUNK, :].rearrange(
@@ -353,6 +368,7 @@ def tile_causalselfattention_pa_t_kernel(
             if i + 2 < CHUNKS:
                 turn(i + 2)
             if 0 <= i < CHUNKS:
+                value(i)
                 add_bias(i)
                 measure(i)
             if i + 1 < CHUNKS:

@@ -25,7 +25,7 @@ CHUNKS = T // CHUNK
 POS = CHUNKS * SUB
 PAIRS = C // 2
 GROUPS = 2 * H * SUB
-X_BUFS = 5
+X_BUFS = 6
 ROUND = 12582912.0
 
 FLOPS = 2 * T * D * 3 * E
@@ -52,9 +52,8 @@ def tile_causalselfattention_pa_t_kernel(
         work = ctx.enter_context(tc.tile_pool(name="work", bufs=2))
         small = ctx.enter_context(tc.tile_pool(name="small", bufs=2))
         ps_t = ctx.enter_context(tc.psum_pool(name="ps_t", bufs=2))
-        ps_qk = ctx.enter_context(tc.psum_pool(name="ps_qk", bufs=3))
-        ps_vt = ctx.enter_context(tc.psum_pool(name="ps_vt", bufs=2))
-        ps_vb = ctx.enter_context(tc.psum_pool(name="ps_vb", bufs=1))
+        ps_qk = ctx.enter_context(tc.psum_pool(name="ps_qk", bufs=4))
+        ps_v = ctx.enter_context(tc.psum_pool(name="ps_v", bufs=2))
         ctx.enter_context(tc.manual_schedule())
 
         x_rows = {}
@@ -193,18 +192,12 @@ def tile_causalselfattention_pa_t_kernel(
 
         spread = ps_qk.tile([P, 4 * E], F32, tag="acc")
         nc.tensor.matmul(out=spread[:], lhsT=ones[:], rhs=vectors[:], start=True, stop=True)
-        bias = const.tile([P, 2 * E], F32)
+        bias = const.tile([P, 3 * E], F32)
         nc.vector.tensor_copy(
-            out=bias[:].rearrange("p (g e j) -> p g e j", e=2, j=PAIRS),
+            out=bias[:, 0 : 2 * E].rearrange("p (g e j) -> p g e j", e=2, j=PAIRS),
             in_=spread[:, 0 : 2 * E].rearrange("p (g j e) -> p g e j", e=2, j=PAIRS),
         )
-        column = ps_vb.tile([P, 4, P], F32, tag="v_back")
-        nc.tensor.matmul(
-            out=column[:, 0, 0:C], lhsT=vectors[:, 2 * E : 3 * E], rhs=ones[:, 0:C],
-            start=True, stop=True,
-        )
-        bias_v = const.tile([P, 1], F32)
-        nc.vector.tensor_copy(out=bias_v[:], in_=column[:, 0, 0:1])
+        nc.vector.tensor_copy(out=bias[:, 2 * E : 3 * E], in_=spread[:, 2 * E : 3 * E])
         gain = const.tile([P, 2, 2, PAIRS], F32)
         nc.vector.tensor_copy(
             out=gain[:],
@@ -235,18 +228,6 @@ def tile_causalselfattention_pa_t_kernel(
             nc.vector.quantize_mx(
                 out=codes[g][:].bitcast(FP8X4), scales=scales[g][:], in_=grouped[g][:]
             )
-            acc_v[g] = []
-            for b in range(SUB // 4):
-                acc = ps_vt.tile([P, 4 * P], F32, tag="v_t")
-                cols = slice(4 * b * P, 4 * (b + 1) * P)
-                nc.tensor.matmul_mx(
-                    out=acc[:],
-                    lhsT=w_codes[:, 2 * E : 3 * E].bitcast(FP8X4),
-                    lhsT_scale=w_scales[:, 2 * E : 3 * E],
-                    rhs=codes[g][:, cols].bitcast(FP8X4), rhs_scale=scales[g][:, cols],
-                    start=True, stop=True,
-                )
-                acc_v[g].append(acc)
             acc_qk[g] = []
             for b in range(SUB // 2):
                 acc = ps_qk.tile([P, 2, 2 * E], F32, tag="acc")
@@ -259,6 +240,19 @@ def tile_causalselfattention_pa_t_kernel(
                         start=True, stop=True,
                     )
                 acc_qk[g].append(acc)
+            acc_v[g] = []
+            for b in range(SUB // 4):
+                acc = ps_v.tile([P, 4, E], F32, tag="acc_v")
+                for s in range(4):
+                    cols = slice((4 * b + s) * P, (4 * b + s + 1) * P)
+                    nc.tensor.matmul_mx(
+                        out=acc[:, s, :],
+                        lhsT=codes[g][:, cols].bitcast(FP8X4), lhsT_scale=scales[g][:, cols],
+                        rhs=w_codes[:, 2 * E : 3 * E].bitcast(FP8X4),
+                        rhs_scale=w_scales[:, 2 * E : 3 * E],
+                        start=True, stop=True,
+                    )
+                acc_v[g].append(acc)
 
         def add_bias(g):
             u_qk[g] = work.tile([P, 2 * H, SUB, C], F32, name="u_qk")
@@ -266,25 +260,16 @@ def tile_causalselfattention_pa_t_kernel(
                 nc.vector.tensor_add(
                     out=u_qk[g][:, :, 2 * b : 2 * b + 2, :],
                     in0=acc_qk[g][b][:].rearrange("p s (g c) -> p g s c", c=C),
-                    in1=bias[:].rearrange("p (g c) -> p g c", c=C).unsqueeze(2)
+                    in1=bias[:, 0 : 2 * E].rearrange("p (g c) -> p g c", c=C).unsqueeze(2)
                     .to_broadcast([P, 2 * H, 2, C]),
-                )
-
-        def value(g):
-            v_turned = work.tile([P, SUB, P], F32)
-            for b in range(SUB // 4):
-                nc.scalar.activation(
-                    out=v_turned[:, 4 * b : 4 * b + 4, :].rearrange("p s m -> p (s m)"),
-                    in_=acc_v[g][b][:], func=ACT.Identity, bias=bias_v[:],
                 )
             v_out = work.tile([P, H, SUB, C], F32)
             for b in range(SUB // 4):
-                v_back = ps_vb.tile([P, 4, P], F32, tag="v_back")
-                for s in range(4):
-                    nc.tensor.transpose(v_back[:, s, :], v_turned[:, 4 * b + s, :], ident[:])
-                nc.scalar.copy(
+                nc.vector.tensor_add(
                     out=v_out[:, :, 4 * b : 4 * b + 4, :],
-                    in_=v_back[:].rearrange("p s (h c) -> p h s c", c=C),
+                    in0=acc_v[g][b][:].rearrange("p s (h c) -> p h s c", c=C),
+                    in1=bias[:, 2 * E : 3 * E].rearrange("p (h c) -> p h c", c=C).unsqueeze(2)
+                    .to_broadcast([P, H, 4, C]),
                 )
             nc.sync.dma_start(
                 out=out_2[:, g * CHUNK : (g + 1) * CHUNK, :].rearrange(
@@ -329,7 +314,7 @@ def tile_causalselfattention_pa_t_kernel(
             normed = u_qk[g][:].rearrange("p g s (e j) -> p (g s) e j", e=2)
             crossed[g] = work.tile([P, GROUPS, 2, PAIRS], F32, name="crossed")
             for e in range(2):
-                nc.gpsimd.tensor_mul(
+                nc.vector.tensor_mul(
                     out=crossed[g][:, :, e, :].rearrange("p (t h s) j -> p t h s j", t=2, h=H),
                     in0=normed[:, :, 1 - e, :].rearrange("p (t h s) j -> p t h s j", t=2, h=H),
                     in1=other[:, e, :, g * SUB : (g + 1) * SUB, :].unsqueeze(2)
@@ -363,12 +348,9 @@ def tile_causalselfattention_pa_t_kernel(
                 )
 
         for i in range(-1, CHUNKS + 1):
-            if 0 <= i - 1:
-                rotate_partner(i - 1)
             if i + 2 < CHUNKS:
                 turn(i + 2)
             if 0 <= i < CHUNKS:
-                value(i)
                 add_bias(i)
                 measure(i)
             if i + 1 < CHUNKS:
@@ -377,5 +359,6 @@ def tile_causalselfattention_pa_t_kernel(
                 invert(i)
                 normalise(i)
             if 0 <= i - 1:
+                rotate_partner(i - 1)
                 rotate_own(i - 1)
                 finish(i - 1)

from contextlib import ExitStack

import concourse.mybir as mybir
from concourse.masks import make_identity

F32 = mybir.dt.float32
BF16 = mybir.dt.bfloat16
I32 = mybir.dt.int32
U32 = mybir.dt.uint32
U8 = mybir.dt.uint8
FP8X4 = mybir.dt.float8_e4m3fn_x4
ALU = mybir.AluOpType
ACT = mybir.ActivationFunctionType

T, D, H, C = 8192, 512, 4, 32
E = H * C
EPS = 1e-6
BASE = 10000.0
PI = 3.141592653589793

P = 128
SUB = 8
CHUNK = P * SUB
CHUNKS = T // CHUNK
POS = CHUNKS * SUB
PAIRS = C // 2
GROUPS = 2 * H * SUB
X_BUFS = 6
ROUND = 12582912.0

FLOPS = 2 * T * D * 3 * E


def split_frequency(pair):
    turns = BASE ** (-pair / PAIRS) / (2.0 * PI)
    scale = 1.0
    while turns * scale < 1024.0:
        scale = scale * 2.0
    high = round(turns * scale) / scale
    return high, turns - high


def tile_causalselfattention_pa_t_kernel(
    tc, x, W_attn, b_attn, q_ln_w, k_ln_w, out_0, out_1, out_2
):
    nc = tc.nc
    with ExitStack() as ctx:
        const = ctx.enter_context(tc.tile_pool(name="const", bufs=1))
        setup = ctx.enter_context(tc.tile_pool(name="setup", bufs=1))
        xpool = ctx.enter_context(tc.tile_pool(name="xpool", bufs=X_BUFS))
        quant = ctx.enter_context(tc.tile_pool(name="quant", bufs=2))
        work = ctx.enter_context(tc.tile_pool(name="work", bufs=2))
        small = ctx.enter_context(tc.tile_pool(name="small", bufs=2))
        ps_t = ctx.enter_context(tc.psum_pool(name="ps_t", bufs=2))
        ps_qk = ctx.enter_context(tc.psum_pool(name="ps_qk", bufs=4))
        ps_v = ctx.enter_context(tc.psum_pool(name="ps_v", bufs=2))
        ctx.enter_context(tc.manual_schedule())

        x_rows = {}
        grouped = {}
        codes = {}
        scales = {}
        acc_qk = {}
        acc_v = {}
        u_qk = {}
        stats = {}
        std = {}
        rstd = {}
        shift = {}
        straight = {}
        crossed = {}

        def load(g):
            x_rows[g] = xpool.tile([P, SUB, D], BF16, name="x_rows")
            nc.sync.dma_start(
                out=x_rows[g][:],
                in_=x[g * CHUNK : (g + 1) * CHUNK, :].rearrange("(p s) k -> p s k", s=SUB),
            )

        def turn(g):
            grouped[g] = quant.tile([P, CHUNK * 4], BF16, align_bytes=64, name="grouped")
            words = grouped[g][:].bitcast(F32).rearrange("p (s m u) -> p s m u", s=SUB, u=2)
            for b in range(SUB // 2):
                xt = ps_t.tile([P, 2, 2, P], F32, tag="xt")
                for s in range(2):
                    for u in range(2):
                        nc.tensor.transpose(
                            xt[:, s, u, :],
                            x_rows[g][:, 2 * b + s, :].bitcast(F32)[:, u * P : (u + 1) * P],
                            ident[:],
                        )
                nc.scalar.copy(
                    out=words[:, 2 * b : 2 * b + 2, :, :],
                    in_=xt[:].rearrange("p s u m -> p s m u"),
                )
            if g + X_BUFS < CHUNKS:
                load(g + X_BUFS)

        load(0)
        w_rows = setup.tile([P, 3, D], BF16)
        nc.sync.dma_start(out=w_rows[:], in_=W_attn.rearrange("(a p) k -> p a k", p=P))
        for g in range(1, X_BUFS):
            load(g)
        vectors = setup.tile([P, 4 * E], BF16)
        nc.vector.memset(vectors[:], 0.0)
        nc.scalar.dma_start(out=vectors[0:1, 0 : 3 * E], in_=b_attn.rearrange("(o n) -> o n", o=1))
        nc.scalar.dma_start(
            out=vectors[0:1, 3 * E : 3 * E + C], in_=q_ln_w.rearrange("(o n) -> o n", o=1)
        )
        nc.scalar.dma_start(
            out=vectors[0:1, 3 * E + C : 3 * E + 2 * C], in_=k_ln_w.rearrange("(o n) -> o n", o=1)
        )
        ones = setup.tile([P, P], BF16)
        nc.vector.memset(ones[:], 1.0)
        eps = const.tile([P, 1], F32)
        nc.vector.memset(eps[:], EPS)
        ident = const.tile([P, P], F32)
        make_identity(nc, ident[:])
        pos_i = setup.tile([P, POS], I32)
        nc.gpsimd.iota(pos_i[:], pattern=[[CHUNK, CHUNKS], [1, SUB]], base=0, channel_multiplier=SUB)

        pos = setup.tile([P, POS], F32)
        nc.vector.tensor_copy(out=pos[:], in_=pos_i[:])
        whole = setup.tile([P, PAIRS, POS], F32)
        for j in range(PAIRS):
            high, low = split_frequency(j)
            nc.vector.tensor_scalar(
                out=whole[:, j, :], in0=pos[:], scalar1=high, scalar2=ROUND,
                op0=ALU.mult, op1=ALU.add,
            )
        nc.vector.tensor_scalar_sub(out=whole[:], in0=whole[:], scalar1=ROUND)
        turns = setup.tile([P, 2, PAIRS, POS], F32)
        for j in range(PAIRS):
            high, low = split_frequency(j)
            nc.vector.scalar_tensor_tensor(
                out=whole[:, j, :], in0=pos[:], scalar=high, in1=whole[:, j, :],
                op0=ALU.mult, op1=ALU.subtract,
            )
            nc.vector.scalar_tensor_tensor(
                out=turns[:, 0, j, :], in0=pos[:], scalar=low, in1=whole[:, j, :],
                op0=ALU.mult, op1=ALU.add,
            )
        nc.vector.tensor_scalar_add(out=turns[:, 1, :, :], in0=turns[:, 0, :, :], scalar1=0.25)
        nearest = setup.tile([P, 2, PAIRS, POS], F32)
        nc.vector.tensor_scalar(
            out=nearest[:], in0=turns[:], scalar1=ROUND, scalar2=ROUND,
            op0=ALU.add, op1=ALU.subtract,
        )
        nc.vector.tensor_sub(out=turns[:], in0=turns[:], in1=nearest[:])
        turn(0)
        trig = setup.tile([P, 2, POS, PAIRS], F32)
        for s in range(2):
            nc.scalar.activation(
                out=trig[:, s, :, :], in_=turns[:, s, :, :].rearrange("p j i -> p i j"),
                func=ACT.Sin, scale=2.0 * PI,
            )

        w_grouped = setup.tile([P, 3 * E * 4], BF16, align_bytes=64)
        w_words = w_grouped[:].bitcast(F32).rearrange("p (a r u) -> p a r u", a=3, u=2)
        w_codes = const.tile([P, 3 * E], U32, align_bytes=64)
        w_scales = const.tile([P, 3 * E], U8, align_bytes=64)
        for a in range(3):
            wt = ps_t.tile([P, 2, 2, P], F32, tag="xt")
            for u in range(2):
                nc.tensor.transpose(
                    wt[:, 0, u, :], w_rows[:, a, :].bitcast(F32)[:, u * P : (u + 1) * P], ident[:]
                )
            if a < 2:
                for e in range(2):
                    nc.vector.tensor_copy(
                        out=w_words[:, a, :, :].rearrange("p (h e j) u -> p h e j u", h=H, e=2)[
                            :, :, e, :, :
                        ],
                        in_=wt[:, 0, :, :].rearrange("p u (h j e) -> p h e j u", h=H, e=2)[
                            :, :, e, :, :
                        ],
                    )
            else:
                nc.vector.tensor_copy(
                    out=w_words[:, a, :, :], in_=wt[:, 0, :, :].rearrange("p u r -> p r u")
                )
        nc.vector.quantize_mx(
            out=w_codes[:, 0 : 2 * E].bitcast(FP8X4),
            scales=w_scales[:, 0 : 2 * E],
            in_=w_grouped[:, 0 : 2 * E * 4],
        )
        nc.vector.quantize_mx(
            out=w_codes[:, 2 * E : 3 * E].bitcast(FP8X4),
            scales=w_scales[:, 2 * E : 3 * E],
            in_=w_grouped[:, 2 * E * 4 : 3 * E * 4],
        )

        spread = ps_qk.tile([P, 4 * E], F32, tag="acc")
        nc.tensor.matmul(out=spread[:], lhsT=ones[:], rhs=vectors[:], start=True, stop=True)
        bias = const.tile([P, 3 * E], F32)
        nc.vector.tensor_copy(
            out=bias[:, 0 : 2 * E].rearrange("p (g e j) -> p g e j", e=2, j=PAIRS),
            in_=spread[:, 0 : 2 * E].rearrange("p (g j e) -> p g e j", e=2, j=PAIRS),
        )
        nc.vector.tensor_copy(out=bias[:, 2 * E : 3 * E], in_=spread[:, 2 * E : 3 * E])
        gain = const.tile([P, 2, 2, PAIRS], F32)
        nc.vector.tensor_copy(
            out=gain[:],
            in_=spread[:, 3 * E : 3 * E + 2 * C].rearrange("p (t j e) -> p t e j", t=2, e=2),
        )
        cross = const.tile([P, 2, 2, PAIRS], F32)
        nc.vector.tensor_scalar_mul(out=cross[:, :, 0, :], in0=gain[:, :, 1, :], scalar1=-1.0)
        nc.vector.tensor_copy(out=cross[:, :, 1, :], in_=gain[:, :, 0, :])

        own = const.tile([P, 2, POS, 2, PAIRS], F32)
        other = const.tile([P, 2, 2, POS, PAIRS], F32)
        for t in range(2):
            for e in range(2):
                nc.gpsimd.tensor_mul(
                    out=other[:, e, t, :, :],
                    in0=trig[:, 0, :, :],
                    in1=cross[:, t, e, :].unsqueeze(1).to_broadcast([P, POS, PAIRS]),
                )
            nc.gpsimd.tensor_mul(
                out=own[:, t, :, :, :],
                in0=trig[:, 1, :, :].unsqueeze(2).to_broadcast([P, POS, 2, PAIRS]),
                in1=gain[:, t, :, :].unsqueeze(1).to_broadcast([P, POS, 2, PAIRS]),
            )

        def project(g):
            codes[g] = quant.tile([P, CHUNK], U32, align_bytes=64, name="codes")
            scales[g] = quant.tile([P, CHUNK], U8, align_bytes=64, name="scales")
            nc.vector.quantize_mx(
                out=codes[g][:].bitcast(FP8X4), scales=scales[g][:], in_=grouped[g][:]
            )
            acc_qk[g] = []
            for b in range(SUB // 2):
                acc = ps_qk.tile([P, 2, 2 * E], F32, tag="acc")
                for s in range(2):
                    cols = slice((2 * b + s) * P, (2 * b + s + 1) * P)
                    nc.tensor.matmul_mx(
                        out=acc[:, s, :],
                        lhsT=codes[g][:, cols].bitcast(FP8X4), lhsT_scale=scales[g][:, cols],
                        rhs=w_codes[:, 0 : 2 * E].bitcast(FP8X4), rhs_scale=w_scales[:, 0 : 2 * E],
                        start=True, stop=True,
                    )
                acc_qk[g].append(acc)
            acc_v[g] = []
            for b in range(SUB // 4):
                acc = ps_v.tile([P, 4, E], F32, tag="acc_v")
                for s in range(4):
                    cols = slice((4 * b + s) * P, (4 * b + s + 1) * P)
                    nc.tensor.matmul_mx(
                        out=acc[:, s, :],
                        lhsT=codes[g][:, cols].bitcast(FP8X4), lhsT_scale=scales[g][:, cols],
                        rhs=w_codes[:, 2 * E : 3 * E].bitcast(FP8X4),
                        rhs_scale=w_scales[:, 2 * E : 3 * E],
                        start=True, stop=True,
                    )
                acc_v[g].append(acc)

        def add_bias(g):
            u_qk[g] = work.tile([P, 2 * H, SUB, C], F32, name="u_qk")
            for b in range(SUB // 2):
                nc.vector.tensor_add(
                    out=u_qk[g][:, :, 2 * b : 2 * b + 2, :],
                    in0=acc_qk[g][b][:].rearrange("p s (g c) -> p g s c", c=C),
                    in1=bias[:, 0 : 2 * E].rearrange("p (g c) -> p g c", c=C).unsqueeze(2)
                    .to_broadcast([P, 2 * H, 2, C]),
                )
            v_out = work.tile([P, H, SUB, C], F32)
            for b in range(SUB // 4):
                nc.vector.tensor_add(
                    out=v_out[:, :, 4 * b : 4 * b + 4, :],
                    in0=acc_v[g][b][:].rearrange("p s (h c) -> p h s c", c=C),
                    in1=bias[:, 2 * E : 3 * E].rearrange("p (h c) -> p h c", c=C).unsqueeze(2)
                    .to_broadcast([P, H, 4, C]),
                )
            nc.sync.dma_start(
                out=out_2[:, g * CHUNK : (g + 1) * CHUNK, :].rearrange(
                    "h (p s) c -> p h (s c)", s=SUB
                ),
                in_=v_out[:].rearrange("p h s c -> p h (s c)"),
            )

        def measure(g):
            pairs_of_groups = u_qk[g][:].rearrange("p g s c -> p (g s) c").rearrange(
                "p (n two) c -> p n c two", two=2
            )
            stats[g] = small.tile([P, GROUPS, 3], F32, name="stats")
            for n in range(GROUPS // 2):
                nc.vector.bn_stats(
                    out=stats[g][:, 2 * n : 2 * n + 2, :].rearrange("p two k -> p (two k)"),
                    in_=pairs_of_groups[:, n, :, :],
                )
            std[g] = small.tile([P, GROUPS], F32, name="std")
            nc.scalar.activation(
                out=std[g][:], in_=stats[g][:, :, 2], func=ACT.Sqrt, scale=1.0 / C, bias=eps[:]
            )

        def invert(g):
            rstd[g] = small.tile([P, GROUPS], F32, name="rstd")
            nc.vector.reciprocal(out=rstd[g][:], in_=std[g][:])
            shift[g] = small.tile([P, GROUPS], F32, name="shift")
            nc.vector.scalar_tensor_tensor(
                out=shift[g][:], in0=stats[g][:, :, 1], scalar=-1.0, in1=rstd[g][:],
                op0=ALU.mult, op1=ALU.mult,
            )

        def normalise(g):
            groups = u_qk[g][:].rearrange("p g s c -> p (g s) c")
            for i in range(GROUPS):
                nc.scalar.activation(
                    out=groups[:, i, :], in_=groups[:, i, :], func=ACT.Identity,
                    scale=rstd[g][:, i : i + 1], bias=shift[g][:, i : i + 1],
                )

        def rotate_partner(g):
            normed = u_qk[g][:].rearrange("p g s (e j) -> p (g s) e j", e=2)
            crossed[g] = work.tile([P, GROUPS, 2, PAIRS], F32, name="crossed")
            for e in range(2):
                nc.vector.tensor_mul(
                    out=crossed[g][:, :, e, :].rearrange("p (t h s) j -> p t h s j", t=2, h=H),
                    in0=normed[:, :, 1 - e, :].rearrange("p (t h s) j -> p t h s j", t=2, h=H),
                    in1=other[:, e, :, g * SUB : (g + 1) * SUB, :].unsqueeze(2)
                    .to_broadcast([P, 2, H, SUB, PAIRS]),
                )

        def rotate_own(g):
            straight[g] = work.tile([P, GROUPS, 2, PAIRS], F32, name="straight")
            nc.vector.tensor_mul(
                out=straight[g][:].rearrange("p (t h s) e j -> p t h (s e j)", t=2, h=H),
                in0=u_qk[g][:].rearrange("p (t h) s c -> p t h (s c)", t=2),
                in1=own[:, :, g * SUB : (g + 1) * SUB, :, :].rearrange("p t s e j -> p t (s e j)")
                .unsqueeze(2).to_broadcast([P, 2, H, SUB * C]),
            )

        def finish(g):
            qk_out = work.tile([P, GROUPS, PAIRS, 2], F32)
            nc.vector.tensor_add(
                out=qk_out[:],
                in0=straight[g][:].rearrange("p i e j -> p i j e"),
                in1=crossed[g][:].rearrange("p i e j -> p i j e"),
            )
            for t, dest in enumerate((out_0, out_1)):
                nc.sync.dma_start(
                    out=dest[:, g * CHUNK : (g + 1) * CHUNK, :].rearrange(
                        "h (p s) c -> p h (s c)", s=SUB
                    ),
                    in_=qk_out[:, t * H * SUB : (t + 1) * H * SUB, :, :].rearrange(
                        "p (h s) j e -> p h (s j e)", h=H
                    ),
                )

        for i in range(-1, CHUNKS + 1):
            if i + 2 < CHUNKS:
                turn(i + 2)
            if 0 <= i < CHUNKS:
                add_bias(i)
                measure(i)
            if i + 1 < CHUNKS:
                project(i + 1)
            if 0 <= i < CHUNKS:
                invert(i)
                normalise(i)
            if 0 <= i - 1:
                rotate_partner(i - 1)
                rotate_own(i - 1)
                finish(i - 1)
